import numpy as np
import ml_dtypes

BF16 = ml_dtypes.bfloat16


def bf(x):
    return np.asarray(x, np.float32).astype(BF16)


def f32(x):
    return np.asarray(x, np.float32)


def f64(x):
    return np.asarray(x).astype(np.float64)


def striped(idx):
    return np.tile(idx.reshape(-1, 16).T, (8, 1))


C, S, N = 1024, 1024, 512


def setup_inputs():
    s = 1.0 / np.sqrt(C)
    return {"x": f32(np.random.standard_normal((C, S))), "xc": f32(np.random.standard_normal((C, N))), "w": bf(np.random.uniform(-s, s, (C, C))), "b": f32(0.5 * np.random.standard_normal((C, 1))), "offs": striped(np.random.permutation(np.tile(np.arange(S), 2))[:N])}


def reference(x, xc, w, b, offs):
    idx = offs[:16].T.reshape(-1)
    d = f64(x)[:, idx] + (-f64(xc))
    return np.maximum(f64(w).T @ (d * d) + f64(b), 0.0)

@@ -1,0 +1,70 @@
+import concourse.mybir as mybir
+from concourse.masks import make_identity
+
+F32, BF16, U16 = mybir.dt.float32, mybir.dt.bfloat16, mybir.dt.uint16
+ADD, MAX = mybir.AluOpType.add, mybir.AluOpType.max
+SQUARE, RELU = mybir.ActivationFunctionType.Square, mybir.ActivationFunctionType.Relu
+
+P = 128
+C = 1024
+S = 1024
+N = 512
+KB = C // P
+MB = C // P
+
+FLOPS = 2 * C * C * N
+
+
+def tile_denseedgemodel_kernel(tc, x, xc, w, b, offs, out):
+    nc = tc.nc
+    with (
+        tc.tile_pool(name="held", bufs=1) as held,
+        tc.psum_pool(name="psum", bufs=MB) as psum,
+    ):
+        offsets = held.tile([P, N // 16], U16, name="offsets")
+        nc.sync.dma_start(offsets[:], offs)
+
+        compare, weights, nodes = [], [], []
+        for k in range(KB):
+            rows = slice(k * P, (k + 1) * P)
+            compare.append(held.tile([P, N], F32, name=f"compare{k}"))
+            nc.sync.dma_start(compare[k][:], xc[rows, :])
+            weights.append(held.tile([P, C], BF16, name=f"weights{k}"))
+            nc.sync.dma_start(weights[k][:], w[rows, :])
+            nodes.append(held.tile([P, S], F32, name=f"nodes{k}"))
+            nc.sync.dma_start(nodes[k][:], x[rows, :])
+
+        bias_rows = held.tile([P, P], F32, name="bias_rows")
+        nc.vector.memset(bias_rows[:], 0.0)
+        nc.sync.dma_start(bias_rows[0:MB, :], b.rearrange("(mb p) o -> mb (p o)", p=P))
+        identity = held.tile([P, P], F32, name="identity")
+        make_identity(nc, identity[:])
+        bias_flipped = psum.tile([P, N], F32, name="bias_flipped", tag="bank")
+        nc.tensor.transpose(bias_flipped[:, 0:P], bias_rows[:], identity[:])
+        bias = held.tile([P, MB], F32, name="bias")
+        nc.vector.tensor_copy(bias[:], bias_flipped[:, 0:MB])
+
+        acc = [psum.tile([P, N], F32, name=f"acc{mb}", tag="bank") for mb in range(MB)]
+        for k in range(KB):
+            negated = held.tile([P, N], F32, name=f"negated{k}")
+            nc.scalar.mul(negated[:], compare[k][:], -1.0)
+            diff = held.tile([P, N], F32, name=f"diff{k}")
+            nc.vector.tensor_tensor(diff[:], nodes[k][:].indirect(offsets[:]), negated[:], ADD)
+            squared = held.tile([P, N], BF16, name=f"squared{k}")
+            nc.scalar.activation(squared[:], diff[:], SQUARE)
+            for mb in range(MB):
+                nc.tensor.matmul(
+                    acc[mb][:],
+                    weights[k][:, mb * P : (mb + 1) * P],
+                    squared[:],
+                    start=(k == 0),
+                    stop=(k == KB - 1),
+                )
+
+        for mb in range(MB):
+            result = held.tile([P, N], F32, name=f"result{mb}")
+            if mb % 2 == 0:
+                nc.scalar.activation(result[:], acc[mb][:], RELU, bias=bias[:, mb : mb + 1])
+            else:
+                nc.vector.tensor_scalar(result[:], acc[mb][:], bias[:, mb : mb + 1], 0.0, op0=ADD, op1=MAX)
+            nc.sync.dma_start(out[mb * P : (mb + 1) * P, :], result[:])

@@ -24,6 +24,16 @@ def tile_denseedgemodel_kernel(tc, x, xc, w, b, offs, out):
         offsets = held.tile([P, N // 16], U16, name="offsets")
         nc.sync.dma_start(offsets[:], offs)
 
+        bias_rows = held.tile([P, P], F32, name="bias_rows")
+        nc.vector.memset(bias_rows[:], 0.0)
+        nc.scalar.dma_start(bias_rows[0:MB, :], b.rearrange("(mb p) o -> mb (p o)", p=P))
+        identity = held.tile([P, P], F32, name="identity")
+        make_identity(nc, identity[:])
+        bias_flipped = psum.tile([P, N], F32, name="bias_flipped", tag="bank")
+        nc.tensor.transpose(bias_flipped[:, 0:P], bias_rows[:], identity[:])
+        bias = held.tile([P, MB], F32, name="bias")
+        nc.vector.tensor_copy(bias[:], bias_flipped[:, 0:MB])
+
         compare, weights, nodes = [], [], []
         for k in range(KB):
             rows = slice(k * P, (k + 1) * P)
@@ -33,16 +43,6 @@ def tile_denseedgemodel_kernel(tc, x, xc, w, b, offs, out):
             nc.sync.dma_start(weights[k][:], w[rows, :])
             nodes.append(held.tile([P, S], F32, name=f"nodes{k}"))
             nc.sync.dma_start(nodes[k][:], x[rows, :])
-
-        bias_rows = held.tile([P, P], F32, name="bias_rows")
-        nc.vector.memset(bias_rows[:], 0.0)
-        nc.sync.dma_start(bias_rows[0:MB, :], b.rearrange("(mb p) o -> mb (p o)", p=P))
-        identity = held.tile([P, P], F32, name="identity")
-        make_identity(nc, identity[:])
-        bias_flipped = psum.tile([P, N], F32, name="bias_flipped", tag="bank")
-        nc.tensor.transpose(bias_flipped[:, 0:P], bias_rows[:], identity[:])
-        bias = held.tile([P, MB], F32, name="bias")
-        nc.vector.tensor_copy(bias[:], bias_flipped[:, 0:MB])
 
         acc = [psum.tile([P, N], F32, name=f"acc{mb}", tag="bank") for mb in range(MB)]
         for k in range(KB):

@@ -11,6 +11,7 @@ S = 1024
 N = 512
 KB = C // P
 MB = C // P
+WARM_UP = 10
 
 FLOPS = 2 * C * C * N
 
@@ -23,6 +24,12 @@ def tile_denseedgemodel_kernel(tc, x, xc, w, b, offs, out):
     ):
         offsets = held.tile([P, N // 16], U16, name="offsets")
         nc.sync.dma_start(offsets[:], offs)
+
+        zeros = held.tile([P, N], BF16, name="zeros")
+        nc.vector.memset(zeros[:], 0.0)
+        warm_up = psum.tile([P, N], F32, name="warm_up", tag="bank")
+        for i in range(WARM_UP):
+            nc.tensor.matmul(warm_up[:], zeros[:, 0:P], zeros[:], start=True, stop=True)
 
         bias_rows = held.tile([P, P], F32, name="bias_rows")
         nc.vector.memset(bias_rows[:], 0.0)

@@ -11,25 +11,23 @@ S = 1024
 N = 512
 KB = C // P
 MB = C // P
-WARM_UP = 10
+PAIR = 2
 
 FLOPS = 2 * C * C * N
 
 
 def tile_denseedgemodel_kernel(tc, x, xc, w, b, offs, out):
     nc = tc.nc
+    x_blocks = x.rearrange("(p k) s -> p k s", k=KB)
+    xc_blocks = xc.rearrange("(p k) j -> p k j", k=KB)
+    w_blocks = w.rearrange("(p k) m -> p k m", k=KB)
+
     with (
         tc.tile_pool(name="held", bufs=1) as held,
         tc.psum_pool(name="psum", bufs=MB) as psum,
     ):
         offsets = held.tile([P, N // 16], U16, name="offsets")
         nc.sync.dma_start(offsets[:], offs)
-
-        zeros = held.tile([P, N], BF16, name="zeros")
-        nc.vector.memset(zeros[:], 0.0)
-        warm_up = psum.tile([P, N], F32, name="warm_up", tag="bank")
-        for i in range(WARM_UP):
-            nc.tensor.matmul(warm_up[:], zeros[:, 0:P], zeros[:], start=True, stop=True)
 
         bias_rows = held.tile([P, P], F32, name="bias_rows")
         nc.vector.memset(bias_rows[:], 0.0)
@@ -41,32 +39,35 @@ def tile_denseedgemodel_kernel(tc, x, xc, w, b, offs, out):
         bias = held.tile([P, MB], F32, name="bias")
         nc.vector.tensor_copy(bias[:], bias_flipped[:, 0:MB])
 
-        compare, weights, nodes = [], [], []
-        for k in range(KB):
-            rows = slice(k * P, (k + 1) * P)
-            compare.append(held.tile([P, N], F32, name=f"compare{k}"))
-            nc.sync.dma_start(compare[k][:], xc[rows, :])
-            weights.append(held.tile([P, C], BF16, name=f"weights{k}"))
-            nc.sync.dma_start(weights[k][:], w[rows, :])
-            nodes.append(held.tile([P, S], F32, name=f"nodes{k}"))
-            nc.sync.dma_start(nodes[k][:], x[rows, :])
-
         acc = [psum.tile([P, N], F32, name=f"acc{mb}", tag="bank") for mb in range(MB)]
-        for k in range(KB):
-            negated = held.tile([P, N], F32, name=f"negated{k}")
-            nc.scalar.mul(negated[:], compare[k][:], -1.0)
-            diff = held.tile([P, N], F32, name=f"diff{k}")
-            nc.vector.tensor_tensor(diff[:], nodes[k][:].indirect(offsets[:]), negated[:], ADD)
-            squared = held.tile([P, N], BF16, name=f"squared{k}")
-            nc.scalar.activation(squared[:], diff[:], SQUARE)
+
+        for first in range(0, KB, PAIR):
+            compare = held.tile([P, PAIR, N], F32, name=f"compare{first}")
+            nc.sync.dma_start(compare[:], xc_blocks[:, first : first + PAIR, :])
+            nodes = []
+            for i in range(PAIR):
+                nodes.append(held.tile([P, S], F32, name=f"nodes{first + i}"))
+                nc.sync.dma_start(nodes[i][:], x_blocks[:, first + i, :])
+            weights = held.tile([P, PAIR, C], BF16, name=f"weights{first}")
+            nc.sync.dma_start(weights[:], w_blocks[:, first : first + PAIR, :])
+
+            negated = held.tile([P, PAIR, N], F32, name=f"negated{first}")
+            nc.vector.tensor_scalar_mul(negated[:], compare[:], -1.0)
+            squared = held.tile([P, PAIR, N], BF16, name=f"squared{first}")
+            for i in range(PAIR):
+                diff = held.tile([P, N], F32, name=f"diff{first + i}")
+                nc.vector.tensor_tensor(diff[:], nodes[i][:].indirect(offsets[:]), negated[:, i, :], ADD)
+                nc.scalar.activation(squared[:, i, :], diff[:], SQUARE)
+
             for mb in range(MB):
-                nc.tensor.matmul(
-                    acc[mb][:],
-                    weights[k][:, mb * P : (mb + 1) * P],
-                    squared[:],
-                    start=(k == 0),
-                    stop=(k == KB - 1),
-                )
+                for i in range(PAIR):
+                    nc.tensor.matmul(
+                        acc[mb][:],
+                        weights[:, i, mb * P : (mb + 1) * P],
+                        squared[:, i, :],
+                        start=(first + i == 0),
+                        stop=(first + i == KB - 1),
+                    )
 
         for mb in range(MB):
             result = held.tile([P, N], F32, name=f"result{mb}")

@@ -11,7 +11,7 @@ S = 1024
 N = 512
 KB = C // P
 MB = C // P
-PAIR = 2
+GROUPS = ((0, 1), (1, 1), (2, 2), (4, 2), (6, 2))
 
 FLOPS = 2 * C * C * N
 
@@ -41,26 +41,26 @@ def tile_denseedgemodel_kernel(tc, x, xc, w, b, offs, out):
 
         acc = [psum.tile([P, N], F32, name=f"acc{mb}", tag="bank") for mb in range(MB)]
 
-        for first in range(0, KB, PAIR):
-            compare = held.tile([P, PAIR, N], F32, name=f"compare{first}")
-            nc.sync.dma_start(compare[:], xc_blocks[:, first : first + PAIR, :])
+        for first, count in GROUPS:
+            compare = held.tile([P, count, N], F32, name=f"compare{first}")
+            nc.sync.dma_start(compare[:], xc_blocks[:, first : first + count, :])
             nodes = []
-            for i in range(PAIR):
+            for i in range(count):
                 nodes.append(held.tile([P, S], F32, name=f"nodes{first + i}"))
                 nc.sync.dma_start(nodes[i][:], x_blocks[:, first + i, :])
-            weights = held.tile([P, PAIR, C], BF16, name=f"weights{first}")
-            nc.sync.dma_start(weights[:], w_blocks[:, first : first + PAIR, :])
+            weights = held.tile([P, count, C], BF16, name=f"weights{first}")
+            nc.sync.dma_start(weights[:], w_blocks[:, first : first + count, :])
 
-            negated = held.tile([P, PAIR, N], F32, name=f"negated{first}")
+            negated = held.tile([P, count, N], F32, name=f"negated{first}")
             nc.vector.tensor_scalar_mul(negated[:], compare[:], -1.0)
-            squared = held.tile([P, PAIR, N], BF16, name=f"squared{first}")
-            for i in range(PAIR):
+            squared = held.tile([P, count, N], BF16, name=f"squared{first}")
+            for i in range(count):
                 diff = held.tile([P, N], F32, name=f"diff{first + i}")
                 nc.vector.tensor_tensor(diff[:], nodes[i][:].indirect(offsets[:]), negated[:, i, :], ADD)
                 nc.scalar.activation(squared[:, i, :], diff[:], SQUARE)
 
             for mb in range(MB):
-                for i in range(PAIR):
+                for i in range(count):
                     nc.tensor.matmul(
                         acc[mb][:],
                         weights[:, i, mb * P : (mb + 1) * P],

@@ -1,5 +1,4 @@
 import concourse.mybir as mybir
-from concourse.masks import make_identity
 
 F32, BF16, U16 = mybir.dt.float32, mybir.dt.bfloat16, mybir.dt.uint16
 ADD, MAX = mybir.AluOpType.add, mybir.AluOpType.max
@@ -28,16 +27,6 @@ def tile_denseedgemodel_kernel(tc, x, xc, w, b, offs, out):
     ):
         offsets = held.tile([P, N // 16], U16, name="offsets")
         nc.sync.dma_start(offsets[:], offs)
-
-        bias_rows = held.tile([P, P], F32, name="bias_rows")
-        nc.vector.memset(bias_rows[:], 0.0)
-        nc.scalar.dma_start(bias_rows[0:MB, :], b.rearrange("(mb p) o -> mb (p o)", p=P))
-        identity = held.tile([P, P], F32, name="identity")
-        make_identity(nc, identity[:])
-        bias_flipped = psum.tile([P, N], F32, name="bias_flipped", tag="bank")
-        nc.tensor.transpose(bias_flipped[:, 0:P], bias_rows[:], identity[:])
-        bias = held.tile([P, MB], F32, name="bias")
-        nc.vector.tensor_copy(bias[:], bias_flipped[:, 0:MB])
 
         acc = [psum.tile([P, N], F32, name=f"acc{mb}", tag="bank") for mb in range(MB)]
 
@@ -68,6 +57,9 @@ def tile_denseedgemodel_kernel(tc, x, xc, w, b, offs, out):
                         start=(first + i == 0),
                         stop=(first + i == KB - 1),
                     )
+
+        bias = held.tile([P, MB], F32, name="bias")
+        nc.sync.dma_start(bias[:], b.rearrange("(mb p) o -> p (mb o)", p=P))
 
         for mb in range(MB):
             result = held.tile([P, N], F32, name=f"result{mb}")

@@ -10,7 +10,8 @@ S = 1024
 N = 512
 KB = C // P
 MB = C // P
-GROUPS = ((0, 1), (1, 1), (2, 2), (4, 2), (6, 2))
+PAIR = 2
+PIECES = ((0, 384), (384, N))
 
 FLOPS = 2 * C * C * N
 
@@ -30,33 +31,45 @@ def tile_denseedgemodel_kernel(tc, x, xc, w, b, offs, out):
 
         acc = [psum.tile([P, N], F32, name=f"acc{mb}", tag="bank") for mb in range(MB)]
 
-        for first, count in GROUPS:
-            compare = held.tile([P, count, N], F32, name=f"compare{first}")
-            nc.sync.dma_start(compare[:], xc_blocks[:, first : first + count, :])
-            nodes = []
-            for i in range(count):
-                nodes.append(held.tile([P, S], F32, name=f"nodes{first + i}"))
-                nc.sync.dma_start(nodes[i][:], x_blocks[:, first + i, :])
-            weights = held.tile([P, count, C], BF16, name=f"weights{first}")
-            nc.sync.dma_start(weights[:], w_blocks[:, first : first + count, :])
+        for first in range(0, KB, PAIR):
+            last = first + PAIR == KB
+            compare = held.tile([P, PAIR, N], F32, name=f"compare{first}")
+            nc.sync.dma_start(compare[:], xc_blocks[:, first : first + PAIR, :])
+            nodes = [held.tile([P, S], F32, name=f"nodes{first + i}") for i in range(PAIR)]
+            weights = held.tile([P, PAIR, C], BF16, name=f"weights{first}")
+            nc.sync.dma_start(nodes[0][:], x_blocks[:, first, :])
+            if not last:
+                nc.sync.dma_start(weights[:], w_blocks[:, first : first + PAIR, :])
+            nc.sync.dma_start(nodes[1][:], x_blocks[:, first + 1, :])
+            if last:
+                nc.sync.dma_start(weights[:], w_blocks[:, first : first + PAIR, :])
 
-            negated = held.tile([P, count, N], F32, name=f"negated{first}")
+            negated = held.tile([P, PAIR, N], F32, name=f"negated{first}")
             nc.vector.tensor_scalar_mul(negated[:], compare[:], -1.0)
-            squared = held.tile([P, count, N], BF16, name=f"squared{first}")
-            for i in range(count):
+            squared = held.tile([P, PAIR, N], BF16, name=f"squared{first}")
+            for i in range(PAIR):
                 diff = held.tile([P, N], F32, name=f"diff{first + i}")
-                nc.vector.tensor_tensor(diff[:], nodes[i][:].indirect(offsets[:]), negated[:, i, :], ADD)
-                nc.scalar.activation(squared[:, i, :], diff[:], SQUARE)
-
-            for mb in range(MB):
-                for i in range(count):
-                    nc.tensor.matmul(
-                        acc[mb][:],
-                        weights[:, i, mb * P : (mb + 1) * P],
-                        squared[:, i, :],
-                        start=(first + i == 0),
-                        stop=(first + i == KB - 1),
+                for begin, end in PIECES:
+                    nc.vector.tensor_tensor(
+                        diff[:, begin:end],
+                        nodes[i][:].indirect(offsets[:, begin // 16 : end // 16]),
+                        negated[:, i, begin:end],
+                        ADD,
                     )
+                    nc.scalar.activation(squared[:, i, begin:end], diff[:, begin:end], SQUARE)
+
+            if last:
+                order = [(mb + j, i) for mb in range(0, MB, 2) for i in range(PAIR) for j in range(2)]
+            else:
+                order = [(mb, i) for i in range(PAIR) for mb in range(MB)]
+            for mb, i in order:
+                nc.tensor.matmul(
+                    acc[mb][:],
+                    weights[:, i, mb * P : (mb + 1) * P],
+                    squared[:, i, :],
+                    start=(first + i == 0),
+                    stop=(first + i == KB - 1),
+                )
 
         bias = held.tile([P, MB], F32, name="bias")
         nc.sync.dma_start(bias[:], b.rearrange("(mb p) o -> p (mb o)", p=P))

@@ -11,7 +11,9 @@ N = 512
 KB = C // P
 MB = C // P
 PAIR = 2
-PIECES = ((0, 384), (384, N))
+HALF = N // 2
+LEFT, RIGHT = slice(0, HALF), slice(HALF, N)
+SPLIT = 2
 
 FLOPS = 2 * C * C * N
 
@@ -24,60 +26,97 @@ def tile_denseedgemodel_kernel(tc, x, xc, w, b, offs, out):
 
     with (
         tc.tile_pool(name="held", bufs=1) as held,
-        tc.psum_pool(name="psum", bufs=MB) as psum,
+        tc.psum_pool(name="psum", bufs=1) as psum,
     ):
         offsets = held.tile([P, N // 16], U16, name="offsets")
         nc.sync.dma_start(offsets[:], offs)
 
-        acc = [psum.tile([P, N], F32, name=f"acc{mb}", tag="bank") for mb in range(MB)]
+        left = psum.tile([P, SPLIT, HALF], F32, name="left")
+        right = psum.tile([P, SPLIT, HALF], F32, name="right")
+        whole = {mb: psum.tile([P, N], F32, name=f"whole{mb}") for mb in range(SPLIT, MB)}
+        weights, squared = [], []
+
+        def multiply(k, mb):
+            nc.tensor.matmul(
+                whole[mb][:],
+                weights[k][:, mb * P : (mb + 1) * P],
+                squared[k][:],
+                start=(k == 0),
+                stop=(k == KB - 1),
+            )
+
+        def multiply_half(k, mb, bank, edges):
+            nc.tensor.matmul(
+                bank[:, mb, :],
+                weights[k][:, mb * P : (mb + 1) * P],
+                squared[k][:, edges],
+                start=(k == 0 and mb == 0),
+                stop=(k == KB - 1 and mb == SPLIT - 1),
+            )
 
         for first in range(0, KB, PAIR):
             last = first + PAIR == KB
             compare = held.tile([P, PAIR, N], F32, name=f"compare{first}")
             nc.sync.dma_start(compare[:], xc_blocks[:, first : first + PAIR, :])
             nodes = [held.tile([P, S], F32, name=f"nodes{first + i}") for i in range(PAIR)]
-            weights = held.tile([P, PAIR, C], BF16, name=f"weights{first}")
+            pair_weights = held.tile([P, PAIR, C], BF16, name=f"weights{first}")
             nc.sync.dma_start(nodes[0][:], x_blocks[:, first, :])
             if not last:
-                nc.sync.dma_start(weights[:], w_blocks[:, first : first + PAIR, :])
+                nc.sync.dma_start(pair_weights[:], w_blocks[:, first : first + PAIR, :])
             nc.sync.dma_start(nodes[1][:], x_blocks[:, first + 1, :])
             if last:
-                nc.sync.dma_start(weights[:], w_blocks[:, first : first + PAIR, :])
+                for i in range(PAIR):
+                    nc.sync.dma_start(pair_weights[:, i, :], w_blocks[:, first + i, :])
 
             negated = held.tile([P, PAIR, N], F32, name=f"negated{first}")
             nc.vector.tensor_scalar_mul(negated[:], compare[:], -1.0)
-            squared = held.tile([P, PAIR, N], BF16, name=f"squared{first}")
             for i in range(PAIR):
                 diff = held.tile([P, N], F32, name=f"diff{first + i}")
-                for begin, end in PIECES:
+                block = held.tile([P, N], BF16, name=f"squared{first + i}")
+                for h, edges in enumerate((LEFT, RIGHT)):
+                    columns = slice(h * HALF // 16, (h + 1) * HALF // 16)
                     nc.vector.tensor_tensor(
-                        diff[:, begin:end],
-                        nodes[i][:].indirect(offsets[:, begin // 16 : end // 16]),
-                        negated[:, i, begin:end],
-                        ADD,
+                        diff[:, edges], nodes[i][:].indirect(offsets[:, columns]), negated[:, i, edges], ADD
                     )
-                    nc.scalar.activation(squared[:, i, begin:end], diff[:, begin:end], SQUARE)
+                    nc.scalar.activation(block[:, edges], diff[:, edges], SQUARE)
+                weights.append(pair_weights[:, i, :])
+                squared.append(block)
 
-            if last:
-                order = [(mb + j, i) for mb in range(0, MB, 2) for i in range(PAIR) for j in range(2)]
-            else:
-                order = [(mb, i) for i in range(PAIR) for mb in range(MB)]
-            for mb, i in order:
-                nc.tensor.matmul(
-                    acc[mb][:],
-                    weights[:, i, mb * P : (mb + 1) * P],
-                    squared[:, i, :],
-                    start=(first + i == 0),
-                    stop=(first + i == KB - 1),
-                )
+            if not last:
+                for k in (first, first + 1):
+                    for mb in range(SPLIT):
+                        multiply_half(k, mb, left, LEFT)
+                        multiply_half(k, mb, right, RIGHT)
+                    for mb in range(SPLIT, MB):
+                        multiply(k, mb)
 
         bias = held.tile([P, MB], F32, name="bias")
         nc.sync.dma_start(bias[:], b.rearrange("(mb p) o -> p (mb o)", p=P))
+        result = [held.tile([P, N], F32, name=f"result{mb}") for mb in range(MB)]
 
-        for mb in range(MB):
-            result = held.tile([P, N], F32, name=f"result{mb}")
-            if mb % 2 == 0:
-                nc.scalar.activation(result[:], acc[mb][:], RELU, bias=bias[:, mb : mb + 1])
+        def finish(engine, mb, accumulator, edges):
+            value = result[mb][:, edges]
+            if engine is nc.scalar:
+                nc.scalar.activation(value, accumulator, RELU, bias=bias[:, mb : mb + 1])
             else:
-                nc.vector.tensor_scalar(result[:], acc[mb][:], bias[:, mb : mb + 1], 0.0, op0=ADD, op1=MAX)
-            nc.sync.dma_start(out[mb * P : (mb + 1) * P, :], result[:])
+                nc.vector.tensor_scalar(value, accumulator, bias[:, mb : mb + 1], 0.0, op0=ADD, op1=MAX)
+            nc.sync.dma_start(out[mb * P : (mb + 1) * P, edges], value)
+
+        for mb in range(SPLIT):
+            multiply_half(KB - 2, mb, left, LEFT)
+            multiply_half(KB - 2, mb, right, RIGHT)
+        for mb in range(SPLIT):
+            multiply_half(KB - 1, mb, left, LEFT)
+        for mb in range(SPLIT):
+            finish(nc.vector, mb, left[:, mb, :], LEFT)
+        multiply(KB - 2, SPLIT)
+        for mb in range(SPLIT):
+            multiply_half(KB - 1, mb, right, RIGHT)
+        for mb in range(SPLIT):
+            finish(nc.scalar, mb, right[:, mb, :], RIGHT)
+        multiply(KB - 1, SPLIT)
+        finish(nc.vector, SPLIT, whole[SPLIT][:], slice(0, N))
+        for mb in range(SPLIT + 1, MB):
+            multiply(KB - 2, mb)
+            multiply(KB - 1, mb)
+            finish(nc.scalar if mb % 2 else nc.vector, mb, whole[mb][:], slice(0, N))

@@ -13,6 +13,7 @@ MB = C // P
 PAIR = 2
 HALF = N // 2
 LEFT, RIGHT = slice(0, HALF), slice(HALF, N)
+SQUARE_SIDE = 32
 SPLIT = 2
 
 FLOPS = 2 * C * C * N
@@ -30,6 +31,9 @@ def tile_denseedgemodel_kernel(tc, x, xc, w, b, offs, out):
     ):
         offsets = held.tile([P, N // 16], U16, name="offsets")
         nc.sync.dma_start(offsets[:], offs)
+
+        bias_rows = held.tile([P, SQUARE_SIDE], F32, name="bias_rows", align_bytes=64)
+        nc.vector.memset(bias_rows[:], 0.0)
 
         left = psum.tile([P, SPLIT, HALF], F32, name="left")
         right = psum.tile([P, SPLIT, HALF], F32, name="right")
@@ -90,8 +94,11 @@ def tile_denseedgemodel_kernel(tc, x, xc, w, b, offs, out):
                     for mb in range(SPLIT, MB):
                         multiply(k, mb)
 
-        bias = held.tile([P, MB], F32, name="bias")
-        nc.sync.dma_start(bias[:], b.rearrange("(mb p) o -> p (mb o)", p=P))
+        b_squares = b.rearrange("(mb g r) o -> g mb (r o)", mb=MB, r=SQUARE_SIDE)
+        for g in range(P // SQUARE_SIDE):
+            nc.sync.dma_start(bias_rows[g * SQUARE_SIDE : g * SQUARE_SIDE + MB, :], b_squares[g])
+        bias = held.tile([P, SQUARE_SIDE], F32, name="bias", align_bytes=64)
+        nc.vector.transpose(bias[:], bias_rows[:])
         result = [held.tile([P, N], F32, name=f"result{mb}") for mb in range(MB)]
 
         def finish(engine, mb, accumulator, edges):

@@ -60,13 +60,14 @@ def tile_denseedgemodel_kernel(tc, x, xc, w, b, offs, out):
 
         for first in range(0, KB, PAIR):
             last = first + PAIR == KB
+            side = nc.scalar if first < KB // 2 else nc.sync
             compare = held.tile([P, PAIR, N], F32, name=f"compare{first}")
-            nc.sync.dma_start(compare[:], xc_blocks[:, first : first + PAIR, :])
+            side.dma_start(compare[:], xc_blocks[:, first : first + PAIR, :])
             nodes = [held.tile([P, S], F32, name=f"nodes{first + i}") for i in range(PAIR)]
             pair_weights = held.tile([P, PAIR, C], BF16, name=f"weights{first}")
             nc.sync.dma_start(nodes[0][:], x_blocks[:, first, :])
             if not last:
-                nc.sync.dma_start(pair_weights[:], w_blocks[:, first : first + PAIR, :])
+                side.dma_start(pair_weights[:], w_blocks[:, first : first + PAIR, :])
             nc.sync.dma_start(nodes[1][:], x_blocks[:, first + 1, :])
             if last:
                 for i in range(PAIR):

import concourse.mybir as mybir

F32, BF16, U16 = mybir.dt.float32, mybir.dt.bfloat16, mybir.dt.uint16
ADD, MAX = mybir.AluOpType.add, mybir.AluOpType.max
SQUARE, RELU = mybir.ActivationFunctionType.Square, mybir.ActivationFunctionType.Relu

P = 128
C = 1024
S = 1024
N = 512
KB = C // P
MB = C // P
PAIR = 2
HALF = N // 2
LEFT, RIGHT = slice(0, HALF), slice(HALF, N)
SQUARE_SIDE = 32
SPLIT = 2

FLOPS = 2 * C * C * N


def tile_denseedgemodel_kernel(tc, x, xc, w, b, offs, out):
    nc = tc.nc
    x_blocks = x.rearrange("(p k) s -> p k s", k=KB)
    xc_blocks = xc.rearrange("(p k) j -> p k j", k=KB)
    w_blocks = w.rearrange("(p k) m -> p k m", k=KB)

    with (
        tc.tile_pool(name="held", bufs=1) as held,
        tc.psum_pool(name="psum", bufs=1) as psum,
    ):
        offsets = held.tile([P, N // 16], U16, name="offsets")
        nc.sync.dma_start(offsets[:], offs)

        bias_rows = held.tile([P, SQUARE_SIDE], F32, name="bias_rows", align_bytes=64)
        nc.vector.memset(bias_rows[:], 0.0)

        left = psum.tile([P, SPLIT, HALF], F32, name="left")
        right = psum.tile([P, SPLIT, HALF], F32, name="right")
        whole = {mb: psum.tile([P, N], F32, name=f"whole{mb}") for mb in range(SPLIT, MB)}
        weights, squared = [], []

        def multiply(k, mb):
            nc.tensor.matmul(
                whole[mb][:],
                weights[k][:, mb * P : (mb + 1) * P],
                squared[k][:],
                start=(k == 0),
                stop=(k == KB - 1),
            )

        def multiply_half(k, mb, bank, edges):
            nc.tensor.matmul(
                bank[:, mb, :],
                weights[k][:, mb * P : (mb + 1) * P],
                squared[k][:, edges],
                start=(k == 0 and mb == 0),
                stop=(k == KB - 1 and mb == SPLIT - 1),
            )

        for first in range(0, KB, PAIR):
            last = first + PAIR == KB
            side = nc.scalar if first < KB // 2 else nc.sync
            compare = held.tile([P, PAIR, N], F32, name=f"compare{first}")
            side.dma_start(compare[:], xc_blocks[:, first : first + PAIR, :])
            nodes = [held.tile([P, S], F32, name=f"nodes{first + i}") for i in range(PAIR)]
            pair_weights = held.tile([P, PAIR, C], BF16, name=f"weights{first}")
            nc.sync.dma_start(nodes[0][:], x_blocks[:, first, :])
            if not last:
                side.dma_start(pair_weights[:], w_blocks[:, first : first + PAIR, :])
            nc.sync.dma_start(nodes[1][:], x_blocks[:, first + 1, :])
            if last:
                for i in range(PAIR):
                    nc.sync.dma_start(pair_weights[:, i, :], w_blocks[:, first + i, :])

            negated = held.tile([P, PAIR, N], F32, name=f"negated{first}")
            nc.vector.tensor_scalar_mul(negated[:], compare[:], -1.0)
            for i in range(PAIR):
                diff = held.tile([P, N], F32, name=f"diff{first + i}")
                block = held.tile([P, N], BF16, name=f"squared{first + i}")
                for h, edges in enumerate((LEFT, RIGHT)):
                    columns = slice(h * HALF // 16, (h + 1) * HALF // 16)
                    nc.vector.tensor_tensor(
                        diff[:, edges], nodes[i][:].indirect(offsets[:, columns]), negated[:, i, edges], ADD
                    )
                    nc.scalar.activation(block[:, edges], diff[:, edges], SQUARE)
                weights.append(pair_weights[:, i, :])
                squared.append(block)

            if not last:
                for k in (first, first + 1):
                    for mb in range(SPLIT):
                        multiply_half(k, mb, left, LEFT)
                        multiply_half(k, mb, right, RIGHT)
                    for mb in range(SPLIT, MB):
                        multiply(k, mb)

        b_squares = b.rearrange("(mb g r) o -> g mb (r o)", mb=MB, r=SQUARE_SIDE)
        for g in range(P // SQUARE_SIDE):
            nc.sync.dma_start(bias_rows[g * SQUARE_SIDE : g * SQUARE_SIDE + MB, :], b_squares[g])
        bias = held.tile([P, SQUARE_SIDE], F32, name="bias", align_bytes=64)
        nc.vector.transpose(bias[:], bias_rows[:])
        result = [held.tile([P, N], F32, name=f"result{mb}") for mb in range(MB)]

        def finish(engine, mb, accumulator, edges):
            value = result[mb][:, edges]
            if engine is nc.scalar:
                nc.scalar.activation(value, accumulator, RELU, bias=bias[:, mb : mb + 1])
            else:
                nc.vector.tensor_scalar(value, accumulator, bias[:, mb : mb + 1], 0.0, op0=ADD, op1=MAX)
            nc.sync.dma_start(out[mb * P : (mb + 1) * P, edges], value)

        for mb in range(SPLIT):
            multiply_half(KB - 2, mb, left, LEFT)
            multiply_half(KB - 2, mb, right, RIGHT)
        for mb in range(SPLIT):
            multiply_half(KB - 1, mb, left, LEFT)
        for mb in range(SPLIT):
            finish(nc.vector, mb, left[:, mb, :], LEFT)
        multiply(KB - 2, SPLIT)
        for mb in range(SPLIT):
            multiply_half(KB - 1, mb, right, RIGHT)
        for mb in range(SPLIT):
            finish(nc.scalar, mb, right[:, mb, :], RIGHT)
        multiply(KB - 1, SPLIT)
        finish(nc.vector, SPLIT, whole[SPLIT][:], slice(0, N))
        for mb in range(SPLIT + 1, MB):
            multiply(KB - 2, mb)
            multiply(KB - 1, mb)
            finish(nc.scalar if mb % 2 else nc.vector, mb, whole[mb][:], slice(0, N))
